import numpy as np
import ml_dtypes


def mxq(x, axis, fmt="e4m3"):
    dtype, down = {"e4m3": (ml_dtypes.float8_e4m3fn, 7), "e5m2": (ml_dtypes.float8_e5m2, 14)}[fmt]
    v = np.moveaxis(np.asarray(x, np.float32).astype(ml_dtypes.bfloat16).astype(np.float64), axis, -1)
    blocks = v.reshape(v.shape[:-1] + (-1, 32))
    amax = np.abs(blocks).max(-1, keepdims=True)
    byte = np.maximum(np.where(amax > 0, np.frexp(amax)[1] - 1 + 127, 0) - down, 1)
    scale = np.exp2(byte - 127.0)
    codes = (blocks / scale).astype(np.float32).astype(dtype).astype(np.float64)
    return np.moveaxis((codes * scale).reshape(v.shape), -1, axis)


WIDE = False


def mx_kscale(k):
    if not WIDE:
        return np.ones(k)
    levels = np.array([10, -10, 5, -5, 0])
    a = np.random.permutation(np.resize(levels, k // 512 * 4)).reshape(k // 512, 4)
    idx = np.arange(k)
    return np.exp2(a[idx // 512, idx % 128 // 32])


BF16 = ml_dtypes.bfloat16


def bf(x):
    return np.asarray(x, np.float32).astype(BF16)


def f64(x):
    return np.asarray(x).astype(np.float64)


B, S, M, H, HKV, DH, R_T, R_H, R_W = 1, 1024, 1536, 12, 2, 128, 16, 24, 24
SECT = (2 * R_T, 2 * R_H, 2 * R_W)
NC = len(SECT)


def rotate_half(x):
    h = x.shape[-1] // 2
    return np.concatenate((-x[..., h:], x[..., :h]), axis=-1)


def mrope_combine(t):
    parts, off = [], 0
    for i, sz in enumerate(SECT):
        parts.append(t[i % NC, :, :, off:off + sz])
        off += sz
    return np.concatenate(parts, axis=-1)


def setup_inputs():
    s = mx_kscale(M)
    sd = 1.0 / np.sqrt(M)
    return {"hidden_states": bf(np.random.standard_normal((B, S, M)) * s),
            "cos": bf(np.random.standard_normal((NC, B, S, DH))),
            "sin": bf(np.random.standard_normal((NC, B, S, DH))),
            "Wq": bf(np.random.standard_normal((M, H, DH)) * sd / s[:, None, None]),
            "bq": bf(np.random.standard_normal((H, DH)) * 0.3),
            "Wk": bf(np.random.standard_normal((M, HKV, DH)) * sd / s[:, None, None]),
            "bk": bf(np.random.standard_normal((HKV, DH)) * 0.3),
            "Wv": bf(np.random.standard_normal((M, HKV, DH)) * sd / s[:, None, None]),
            "bv": bf(np.random.standard_normal((HKV, DH)) * 0.3)}


def reference(hidden_states, cos, sin, Wq, bq, Wk, bk, Wv, bv):
    xq = mxq(f64(hidden_states), 2, "e4m3")
    q = (xq @ mxq(f64(Wq).reshape(M, H * DH), 0, "e4m3")).reshape(B, S, H, DH) + f64(bq)
    k = (xq @ mxq(f64(Wk).reshape(M, HKV * DH), 0, "e4m3")).reshape(B, S, HKV, DH) + f64(bk)
    v = (xq @ mxq(f64(Wv).reshape(M, HKV * DH), 0, "e4m3")).reshape(B, S, HKV, DH) + f64(bv)
    cos_c = mrope_combine(f64(cos))[:, :, None, :]
    sin_c = mrope_combine(f64(sin))[:, :, None, :]
    q_rot = q * cos_c + rotate_half(q) * sin_c
    k_rot = k * cos_c + rotate_half(k) * sin_c
    return q_rot, k_rot, v

@@ -1,0 +1,294 @@
+from contextlib import ExitStack
+
+import concourse.mybir as mybir
+from concourse.masks import make_identity
+
+F32 = mybir.dt.float32
+BF16 = mybir.dt.bfloat16
+U32 = mybir.dt.uint32
+U8 = mybir.dt.uint8
+FP8X4 = mybir.dt.float8_e4m3fn_x4
+ADD = mybir.AluOpType.add
+MULT = mybir.AluOpType.mult
+ACT = mybir.ActivationFunctionType
+
+P = 128
+S = 1024
+M = 1536
+PASSES = 3
+T8 = 8
+
+FLOPS = 2 * S * M * 2048
+BYTES = S * M * 2 + M * 2048 * 2 + 16 * 128 * 2 + 2 * S * 128 * 2 + S * 2048 * 4
+
+COS_PARTS = ((0, 0, 32, 0), (1, 32, 80, 32), (2, 80, 128, 80))
+SIN_PARTS = ((1, 64, 80, 0), (2, 80, 128, 16), (0, 0, 32, 64), (1, 32, 64, 96))
+
+
+def tile_qwen2vlattention_pa_kernel(
+    tc, hidden_states, cos, sin, Wq, bq, Wk, bk, Wv, bv, out_0, out_1, out_2
+):
+    nc = tc.nc
+    x_v = hidden_states.rearrange("b s m -> (b s) m").rearrange("(p t) m -> p t m", t=T8)
+    cos_v = cos.rearrange("c b s d -> c (b s) d")
+    sin_v = sin.rearrange("c b s d -> c (b s) d")
+    wq_v = Wq.rearrange("m h d -> m (h d)")
+    wk_v = Wk.rearrange("m h d -> m (h d)")
+    wv_v = Wv.rearrange("m h d -> m (h d)")
+    o0_v = out_0.rearrange("b s h d -> (b s) (h d)").rearrange("(p t) n -> p t n", t=T8)
+    o1_v = out_1.rearrange("b s h d -> (b s) (h d)").rearrange("(p t) n -> p t n", t=T8)
+    o2_v = out_2.rearrange("b s h d -> (b s) (h d)").rearrange("(p t) n -> p t n", t=T8)
+
+    with ExitStack() as ctx:
+        keep = ctx.enter_context(tc.tile_pool(name="keep", bufs=1))
+        xgp = ctx.enter_context(tc.tile_pool(name="xgp", bufs=3))
+        wgp = ctx.enter_context(tc.tile_pool(name="wgp", bufs=4))
+        uwp = ctx.enter_context(tc.tile_pool(name="uwp", bufs=2))
+        outp = ctx.enter_context(tc.tile_pool(name="outp", bufs=6))
+        psum = ctx.enter_context(tc.psum_pool(name="psum", bufs=1))
+        ctx.enter_context(tc.manual_schedule())
+
+        def bank(i, shape, dtype):
+            return psum.tile(shape, dtype, name="bank%d" % i, tag="bank%d" % i)
+
+        ident_f = keep.tile([P, P], F32, name="ident_f")
+        ident_b = keep.tile([P, P], BF16, name="ident_b")
+        perm_f = keep.tile([P, P], F32, name="perm_f")
+        sgn = keep.tile([P, 1], F32, name="sgn")
+        b_raw = keep.tile([P, P], BF16, name="b_raw")
+        b_t = keep.tile([P, 16], F32, name="b_t")
+        c_raw = keep.tile([P, T8, P], BF16, name="c_raw")
+        s_raw = keep.tile([P, T8, P], BF16, name="s_raw")
+        cos_t = keep.tile([P, S], BF16, name="cos_t")
+        sin_t = keep.tile([P, S], BF16, name="sin_t")
+        x_raw = keep.tile([P, T8 * M], BF16, name="x_raw")
+        xq = keep.tile([P, 2, PASSES, 512], U32, name="xq", align_bytes=64)
+        xs = keep.tile([P, 2, PASSES, 512], U8, name="xs", align_bytes=64)
+        wq = [keep.tile([P, PASSES, 512], U32, name="wq%d" % c, align_bytes=64) for c in range(4)]
+        ws = [keep.tile([P, PASSES, 512], U8, name="ws%d" % c, align_bytes=64) for c in range(4)]
+        w_raw = [
+            [keep.tile([P, 4, 512], BF16, name="wraw%d_%d" % (c, g)) for g in range(PASSES)]
+            for c in range(4)
+        ]
+        x_w = x_raw[:].bitcast(F32)
+
+        make_identity(nc, ident_f[:])
+        make_identity(nc, ident_b[:])
+        nc.vector.memset(b_raw[:], 0.0)
+        nc.vector.memset(sgn[0:64, :], 1.0)
+        nc.vector.memset(sgn[64:128, :], -1.0)
+        nc.vector.tensor_copy(out=perm_f[:, 0:64], in_=ident_f[:, 64:128])
+        nc.vector.tensor_copy(out=perm_f[:, 64:128], in_=ident_f[:, 0:64])
+
+        def load_x(t8):
+            nc.sync.dma_start(out=x_raw[:, t8 * M : (t8 + 1) * M], in_=x_v[:, t8, :])
+
+        def load_w(c):
+            for g in range(PASSES):
+                for u in range(2):
+                    rows = slice(512 * g + 256 * u, 512 * g + 256 * u + 256)
+                    dst = w_raw[c][g]
+                    if c < 3:
+                        nc.sync.dma_start(
+                            out=dst[:, 2 * u : 2 * u + 2, :],
+                            in_=wq_v[rows, 512 * c : 512 * c + 512].rearrange("(q e) n -> q e n", e=2),
+                        )
+                    else:
+                        nc.sync.dma_start(
+                            out=dst[:, 2 * u : 2 * u + 2, 0:256],
+                            in_=wk_v[rows, :].rearrange("(q e) n -> q e n", e=2),
+                        )
+                        nc.sync.dma_start(
+                            out=dst[:, 2 * u : 2 * u + 2, 256:512],
+                            in_=wv_v[rows, :].rearrange("(q e) n -> q e n", e=2),
+                        )
+
+        def load_tables(half):
+            ts = slice(4 * half, 4 * half + 4)
+            for comp, lo, hi, dlo in COS_PARTS:
+                src = cos_v[comp].rearrange("(p t) d -> p t d", t=T8)
+                nc.sync.dma_start(out=c_raw[:, ts, dlo : dlo + hi - lo], in_=src[:, ts, lo:hi])
+            for comp, lo, hi, dlo in SIN_PARTS:
+                src = sin_v[comp].rearrange("(p t) d -> p t d", t=T8)
+                nc.sync.dma_start(out=s_raw[:, ts, dlo : dlo + hi - lo], in_=src[:, ts, lo:hi])
+
+        for t8 in range(4):
+            load_x(t8)
+        load_w(0)
+        nc.sync.dma_start(out=b_raw[0:12, :], in_=bq)
+        nc.sync.dma_start(out=b_raw[12:14, :], in_=bk)
+        nc.sync.dma_start(out=b_raw[14:16, :], in_=bv)
+        load_tables(0)
+        for t8 in range(4, 8):
+            load_x(t8)
+        load_tables(1)
+        load_w(1)
+        load_w(2)
+        load_w(3)
+
+        xg = {}
+        wg = {}
+        accs = {}
+        us = {}
+        wss = {}
+
+        def x_transposes(half, banks):
+            for g in range(PASSES):
+                grouped = xgp.tile([P, 2048], BF16, name="xg", tag="xg", align_bytes=64)
+                xg[(half, g)] = grouped
+                words = grouped[:].bitcast(F32).rearrange("p (tt s u) -> p tt s u", tt=4, u=2)
+                for tp in range(2):
+                    xt = bank(banks[2 * g + tp], [P, 2, 2, P], F32)
+                    for tt in range(2):
+                        for u in range(2):
+                            col = (4 * half + 2 * tp + tt) * (M // 2) + 256 * g + 128 * u
+                            nc.tensor.transpose(xt[:, tt, u, :], x_w[:, col : col + P], ident_f[:])
+                    nc.scalar.copy(
+                        out=words[:, 2 * tp : 2 * tp + 2],
+                        in_=xt[:].rearrange("p tt u s -> p tt s u"),
+                    )
+
+        def quant_x(half, g):
+            nc.vector.quantize_mx(
+                out=xq[:, half, g, :].bitcast(FP8X4), scales=xs[:, half, g, :], in_=xg[(half, g)][:]
+            )
+
+        def regroup(on_vector, c, g):
+            grouped = wgp.tile([P, 2048], BF16, name="wg", tag="wg", align_bytes=64)
+            wg[(c, g)] = grouped
+            dst = grouped[:].rearrange("p (c i t) -> p c t i", i=4, t=4)
+            src = w_raw[c][g][:].rearrange("p t (c i) -> p c t i", i=4)
+            if on_vector:
+                nc.vector.tensor_copy(out=dst, in_=src)
+            else:
+                nc.scalar.copy(out=dst, in_=src)
+
+        def quant_w(c, g):
+            nc.vector.quantize_mx(
+                out=wq[c][:, g, :].bitcast(FP8X4), scales=ws[c][:, g, :], in_=wg[(c, g)][:]
+            )
+
+        def project(r, banks, g_outer):
+            c, half = divmod(r, 2)
+            tiles = [bank(b, [P, 512], F32) for b in banks]
+            accs[r] = tiles
+            if g_outer:
+                order = [(g, hh) for g in range(PASSES) for hh in range(4)]
+            else:
+                order = [(g, hh) for hh in range(4) for g in range(PASSES)]
+            for g, hh in order:
+                cols = slice(P * hh, P * hh + P)
+                nc.tensor.matmul_mx(
+                    out=tiles[hh][:],
+                    lhsT=wq[c][:, g, cols].bitcast(FP8X4),
+                    lhsT_scale=ws[c][:, g, cols],
+                    rhs=xq[:, half, g, :].bitcast(FP8X4),
+                    rhs_scale=xs[:, half, g, :],
+                    start=(g == 0),
+                    stop=(g == PASSES - 1),
+                )
+
+        def bias_transpose(b):
+            bt = bank(b, [P, P], BF16)
+            nc.tensor.transpose(bt[:], b_raw[:], ident_b[:])
+            nc.vector.tensor_copy(out=b_t[:], in_=bt[:, 0:16])
+
+        def table_transposes(half, b):
+            tb = bank(b, [P, 2, 512], BF16)
+            for t in range(4):
+                nc.tensor.transpose(tb[:, 0, P * t : P * t + P], c_raw[:, 4 * half + t, :], ident_b[:])
+            for t in range(4):
+                nc.tensor.transpose(tb[:, 1, P * t : P * t + P], s_raw[:, 4 * half + t, :], ident_b[:])
+            cols = slice(512 * half, 512 * half + 512)
+            nc.scalar.copy(out=cos_t[:, cols], in_=tb[:, 0, :])
+            nc.scalar.activation(out=sin_t[:, cols], in_=tb[:, 1, :], func=ACT.Copy, scale=sgn[:, 0:1])
+
+        def rope(r, extras):
+            c, half = divmod(r, 2)
+            cols = slice(512 * half, 512 * half + 512)
+            us[r] = []
+            wss[r] = []
+            for hh in range(4):
+                h = 4 * c + hh
+                acc = accs[r][hh]
+                u_t = uwp.tile([P, 512], F32, name="u%d" % hh, tag="u%d" % hh)
+                us[r].append(u_t)
+                if h < 14:
+                    w_t = uwp.tile([P, 512], F32, name="w%d" % hh, tag="w%d" % hh)
+                    wss[r].append(w_t)
+                    nc.vector.scalar_tensor_tensor(
+                        out=u_t[:], in0=acc[:], scalar=b_t[:, h : h + 1], in1=cos_t[:, cols], op0=ADD, op1=MULT
+                    )
+                    nc.vector.scalar_tensor_tensor(
+                        out=w_t[:], in0=acc[:], scalar=b_t[:, h : h + 1], in1=sin_t[:, cols], op0=ADD, op1=MULT
+                    )
+                else:
+                    nc.scalar.activation(out=u_t[:], in_=acc[:], func=ACT.Identity, bias=b_t[:, h : h + 1])
+                for extra in extras[hh]:
+                    extra()
+
+        def back(r):
+            c, half = divmod(r, 2)
+            for t in range(4):
+                o_ps = bank(t, [P, 512], F32)
+                blk = slice(P * t, P * t + P)
+                for hh in range(4):
+                    dst = o_ps[:, P * hh : P * hh + P]
+                    if 4 * c + hh < 14:
+                        nc.tensor.matmul(
+                            out=dst, lhsT=us[r][hh][:, blk], rhs=ident_f[:], is_transpose=True, start=True, stop=False
+                        )
+                        nc.tensor.matmul(
+                            out=dst, lhsT=wss[r][hh][:, blk], rhs=perm_f[:], is_transpose=True, start=False, stop=True
+                        )
+                    else:
+                        nc.tensor.transpose(dst, us[r][hh][:, blk], ident_f[:])
+                o_sb = outp.tile([P, 512], F32, name="o_sb", tag="o_sb")
+                nc.scalar.copy(out=o_sb[:], in_=o_ps[:])
+                t8 = 4 * half + t
+                if c < 3:
+                    nc.sync.dma_start(out=o0_v[:, t8, 512 * c : 512 * c + 512], in_=o_sb[:])
+                else:
+                    nc.sync.dma_start(out=o1_v[:, t8, :], in_=o_sb[:, 0:256])
+                    nc.sync.dma_start(out=o2_v[:, t8, :], in_=o_sb[:, 256:512])
+
+        x_transposes(0, (0, 1, 2, 3, 4, 5))
+        regroup(True, 0, 0)
+        quant_x(0, 0)
+        regroup(True, 0, 1)
+        quant_x(0, 1)
+        quant_w(0, 0)
+        regroup(True, 0, 2)
+        quant_x(0, 2)
+        quant_w(0, 1)
+        quant_w(0, 2)
+        project(0, (0, 1, 2, 3), True)
+        bias_transpose(6)
+        table_transposes(0, 7)
+        x_transposes(1, (4, 5, 6, 7, 4, 5))
+        table_transposes(1, 6)
+        rope(0, [[], [lambda: quant_x(1, 0)], [lambda: quant_x(1, 1)], [lambda: quant_x(1, 2)]])
+        project(1, (4, 5, 6, 7), False)
+
+        s_pre = {
+            0: [(1, 0), (1, 2)],
+            1: [(2, 0), (2, 1)],
+            2: [(2, 2)],
+            3: [(3, 0), (3, 1)],
+            4: [(3, 2)],
+        }
+        v_mix = {
+            0: [[lambda: regroup(True, 1, 1)], [lambda: quant_w(1, 0)], [lambda: quant_w(1, 1)], [lambda: quant_w(1, 2)]],
+            1: [[], [lambda: quant_w(2, 0)], [], [lambda: quant_w(2, 1)]],
+            2: [[lambda: quant_w(2, 2)], [], [], []],
+            3: [[], [lambda: quant_w(3, 0)], [], [lambda: quant_w(3, 1)]],
+            4: [[lambda: quant_w(3, 2)], [], [], []],
+        }
+        for r in range(8):
+            for c, g in s_pre.get(r, []):
+                regroup(False, c, g)
+            back(r)
+            if r + 1 < 8:
+                rope(r + 1, v_mix.get(r, [[], [], [], []]))
+            if r + 2 < 8:
+                project(r + 2, (4, 5, 6, 7), False)

@@ -17,6 +17,7 @@ S = 1024
 M = 1536
 PASSES = 3
 T8 = 8
+HALF = 512
 
 FLOPS = 2 * S * M * 2048
 BYTES = S * M * 2 + M * 2048 * 2 + 16 * 128 * 2 + 2 * S * 128 * 2 + S * 2048 * 4
@@ -44,7 +45,7 @@ def tile_qwen2vlattention_pa_kernel(
         xgp = ctx.enter_context(tc.tile_pool(name="xgp", bufs=3))
         wgp = ctx.enter_context(tc.tile_pool(name="wgp", bufs=4))
         uwp = ctx.enter_context(tc.tile_pool(name="uwp", bufs=2))
-        outp = ctx.enter_context(tc.tile_pool(name="outp", bufs=6))
+        outp = ctx.enter_context(tc.tile_pool(name="outp", bufs=8))
         psum = ctx.enter_context(tc.psum_pool(name="psum", bufs=1))
         ctx.enter_context(tc.manual_schedule())
 
@@ -59,16 +60,17 @@ def tile_qwen2vlattention_pa_kernel(
         b_t = keep.tile([P, 16], F32, name="b_t")
         c_raw = keep.tile([P, T8, P], BF16, name="c_raw")
         s_raw = keep.tile([P, T8, P], BF16, name="s_raw")
-        cos_t = keep.tile([P, S], BF16, name="cos_t")
-        sin_t = keep.tile([P, S], BF16, name="sin_t")
+        tab_t = keep.tile([P, 2, 2, HALF], BF16, name="tab_t")
         x_raw = keep.tile([P, T8 * M], BF16, name="x_raw")
-        xq = keep.tile([P, 2, PASSES, 512], U32, name="xq", align_bytes=64)
-        xs = keep.tile([P, 2, PASSES, 512], U8, name="xs", align_bytes=64)
-        wq = [keep.tile([P, PASSES, 512], U32, name="wq%d" % c, align_bytes=64) for c in range(4)]
-        ws = [keep.tile([P, PASSES, 512], U8, name="ws%d" % c, align_bytes=64) for c in range(4)]
+        xq = keep.tile([P, 2, PASSES, HALF], U32, name="xq", align_bytes=64)
+        xs = keep.tile([P, 2, PASSES, HALF], U8, name="xs", align_bytes=64)
+        wq = [keep.tile([P, PASSES, 512], U32, name="wq%d" % j, align_bytes=64) for j in range(4)]
+        ws = [keep.tile([P, PASSES, 512], U8, name="ws%d" % j, align_bytes=64) for j in range(4)]
         w_raw = [
-            [keep.tile([P, 4, 512], BF16, name="wraw%d_%d" % (c, g)) for g in range(PASSES)]
-            for c in range(4)
+            [keep.tile([P, 2, 4, 256], BF16, name="wraw%d_%d" % (j, g)) for g in range(PASSES)]
+            if j == 0
+            else [keep.tile([P, 1, 4, 512], BF16, name="wraw%d_%d" % (j, g)) for g in range(PASSES)]
+            for j in range(4)
         ]
         x_w = x_raw[:].bitcast(F32)
 
@@ -80,27 +82,26 @@ def tile_qwen2vlattention_pa_kernel(
         nc.vector.tensor_copy(out=perm_f[:, 0:64], in_=ident_f[:, 64:128])
         nc.vector.tensor_copy(out=perm_f[:, 64:128], in_=ident_f[:, 0:64])
 
-        def load_x(t8):
-            nc.sync.dma_start(out=x_raw[:, t8 * M : (t8 + 1) * M], in_=x_v[:, t8, :])
+        def load_x(half):
+            for tp in range(2):
+                t8 = 4 * half + 2 * tp
+                nc.sync.dma_start(
+                    out=x_raw[:, t8 * M : (t8 + 2) * M],
+                    in_=x_v[:, t8 : t8 + 2, :].rearrange("p t m -> p (t m)"),
+                )
 
-        def load_w(c):
+        def load_w(j):
             for g in range(PASSES):
                 for u in range(2):
                     rows = slice(512 * g + 256 * u, 512 * g + 256 * u + 256)
-                    dst = w_raw[c][g]
-                    if c < 3:
-                        nc.sync.dma_start(
-                            out=dst[:, 2 * u : 2 * u + 2, :],
-                            in_=wq_v[rows, 512 * c : 512 * c + 512].rearrange("(q e) n -> q e n", e=2),
-                        )
+                    if j == 0:
+                        sources = (wk_v[rows, :], wv_v[rows, :])
                     else:
+                        sources = (wq_v[rows, 512 * (j - 1) : 512 * j],)
+                    for blk, src in enumerate(sources):
                         nc.sync.dma_start(
-                            out=dst[:, 2 * u : 2 * u + 2, 0:256],
-                            in_=wk_v[rows, :].rearrange("(q e) n -> q e n", e=2),
-                        )
-                        nc.sync.dma_start(
-                            out=dst[:, 2 * u : 2 * u + 2, 256:512],
-                            in_=wv_v[rows, :].rearrange("(q e) n -> q e n", e=2),
+                            out=w_raw[j][g][:, blk, 2 * u : 2 * u + 2, :],
+                            in_=src.rearrange("(q e) n -> q e n", e=2),
                         )
 
         def load_tables(half):
@@ -112,16 +113,14 @@ def tile_qwen2vlattention_pa_kernel(
                 src = sin_v[comp].rearrange("(p t) d -> p t d", t=T8)
                 nc.sync.dma_start(out=s_raw[:, ts, dlo : dlo + hi - lo], in_=src[:, ts, lo:hi])
 
-        for t8 in range(4):
-            load_x(t8)
+        load_x(0)
         load_w(0)
         nc.sync.dma_start(out=b_raw[0:12, :], in_=bq)
         nc.sync.dma_start(out=b_raw[12:14, :], in_=bk)
         nc.sync.dma_start(out=b_raw[14:16, :], in_=bv)
         load_tables(0)
-        for t8 in range(4, 8):
-            load_x(t8)
         load_tables(1)
+        load_x(1)
         load_w(1)
         load_w(2)
         load_w(3)
@@ -129,22 +128,29 @@ def tile_qwen2vlattention_pa_kernel(
         xg = {}
         wg = {}
         accs = {}
-        us = {}
-        wss = {}
+        uws = {}
+
+        def bias_column(j, hh):
+            return 12 + hh if j == 0 else 4 * (j - 1) + hh
+
+        def rotated(j, hh):
+            return j > 0 or hh < 2
 
         def x_transposes(half, banks):
+            words = []
             for g in range(PASSES):
                 grouped = xgp.tile([P, 2048], BF16, name="xg", tag="xg", align_bytes=64)
                 xg[(half, g)] = grouped
-                words = grouped[:].bitcast(F32).rearrange("p (tt s u) -> p tt s u", tt=4, u=2)
-                for tp in range(2):
-                    xt = bank(banks[2 * g + tp], [P, 2, 2, P], F32)
+                words.append(grouped[:].bitcast(F32).rearrange("p (tt s u) -> p tt s u", tt=4, u=2))
+            for tp in range(2):
+                for g in range(PASSES):
+                    xt = bank(banks[PASSES * tp + g], [P, 2, 2, P], F32)
                     for tt in range(2):
                         for u in range(2):
                             col = (4 * half + 2 * tp + tt) * (M // 2) + 256 * g + 128 * u
                             nc.tensor.transpose(xt[:, tt, u, :], x_w[:, col : col + P], ident_f[:])
                     nc.scalar.copy(
-                        out=words[:, 2 * tp : 2 * tp + 2],
+                        out=words[g][:, 2 * tp : 2 * tp + 2],
                         in_=xt[:].rearrange("p tt u s -> p tt s u"),
                     )
 
@@ -153,26 +159,28 @@ def tile_qwen2vlattention_pa_kernel(
                 out=xq[:, half, g, :].bitcast(FP8X4), scales=xs[:, half, g, :], in_=xg[(half, g)][:]
             )
 
-        def regroup(on_vector, c, g):
+        def regroup(on_vector, j, g):
             grouped = wgp.tile([P, 2048], BF16, name="wg", tag="wg", align_bytes=64)
-            wg[(c, g)] = grouped
-            dst = grouped[:].rearrange("p (c i t) -> p c t i", i=4, t=4)
-            src = w_raw[c][g][:].rearrange("p t (c i) -> p c t i", i=4)
-            if on_vector:
-                nc.vector.tensor_copy(out=dst, in_=src)
-            else:
-                nc.scalar.copy(out=dst, in_=src)
+            wg[(j, g)] = grouped
+            blocks = w_raw[j][g].shape[1]
+            dst = grouped[:].rearrange("p (b c i t) -> p b c t i", b=blocks, i=4, t=4)
+            src = w_raw[j][g][:].rearrange("p b t (c i) -> p b c t i", i=4)
+            for blk in range(blocks):
+                if on_vector:
+                    nc.vector.tensor_copy(out=dst[:, blk], in_=src[:, blk])
+                else:
+                    nc.scalar.copy(out=dst[:, blk], in_=src[:, blk])
 
-        def quant_w(c, g):
+        def quant_w(j, g):
             nc.vector.quantize_mx(
-                out=wq[c][:, g, :].bitcast(FP8X4), scales=ws[c][:, g, :], in_=wg[(c, g)][:]
+                out=wq[j][:, g, :].bitcast(FP8X4), scales=ws[j][:, g, :], in_=wg[(j, g)][:]
             )
 
-        def project(r, banks, g_outer):
-            c, half = divmod(r, 2)
-            tiles = [bank(b, [P, 512], F32) for b in banks]
+        def project(r, banks, pass_outer):
+            j, half = divmod(r, 2)
+            tiles = [bank(b, [P, HALF], F32) for b in banks]
             accs[r] = tiles
-            if g_outer:
+            if pass_outer:
                 order = [(g, hh) for g in range(PASSES) for hh in range(4)]
             else:
                 order = [(g, hh) for hh in range(4) for g in range(PASSES)]
@@ -180,8 +188,8 @@ def tile_qwen2vlattention_pa_kernel(
                 cols = slice(P * hh, P * hh + P)
                 nc.tensor.matmul_mx(
                     out=tiles[hh][:],
-                    lhsT=wq[c][:, g, cols].bitcast(FP8X4),
-                    lhsT_scale=ws[c][:, g, cols],
+                    lhsT=wq[j][:, g, cols].bitcast(FP8X4),
+                    lhsT_scale=ws[j][:, g, cols],
                     rhs=xq[:, half, g, :].bitcast(FP8X4),
                     rhs_scale=xs[:, half, g, :],
                     start=(g == 0),
@@ -194,63 +202,63 @@ def tile_qwen2vlattention_pa_kernel(
             nc.vector.tensor_copy(out=b_t[:], in_=bt[:, 0:16])
 
         def table_transposes(half, b):
-            tb = bank(b, [P, 2, 512], BF16)
+            tb = bank(b, [P, 2, HALF], BF16)
             for t in range(4):
                 nc.tensor.transpose(tb[:, 0, P * t : P * t + P], c_raw[:, 4 * half + t, :], ident_b[:])
             for t in range(4):
                 nc.tensor.transpose(tb[:, 1, P * t : P * t + P], s_raw[:, 4 * half + t, :], ident_b[:])
-            cols = slice(512 * half, 512 * half + 512)
-            nc.scalar.copy(out=cos_t[:, cols], in_=tb[:, 0, :])
-            nc.scalar.activation(out=sin_t[:, cols], in_=tb[:, 1, :], func=ACT.Copy, scale=sgn[:, 0:1])
+            nc.scalar.copy(out=tab_t[:, half, 0, :], in_=tb[:, 0, :])
+            nc.scalar.activation(out=tab_t[:, half, 1, :], in_=tb[:, 1, :], func=ACT.Copy, scale=sgn[:, 0:1])
 
         def rope(r, extras):
-            c, half = divmod(r, 2)
-            cols = slice(512 * half, 512 * half + 512)
-            us[r] = []
-            wss[r] = []
+            j, half = divmod(r, 2)
+            uws[r] = []
             for hh in range(4):
-                h = 4 * c + hh
+                col = bias_column(j, hh)
                 acc = accs[r][hh]
-                u_t = uwp.tile([P, 512], F32, name="u%d" % hh, tag="u%d" % hh)
-                us[r].append(u_t)
-                if h < 14:
-                    w_t = uwp.tile([P, 512], F32, name="w%d" % hh, tag="w%d" % hh)
-                    wss[r].append(w_t)
+                uw = uwp.tile([P, 2, HALF], F32, name="uw%d" % hh, tag="uw%d" % hh)
+                uws[r].append(uw)
+                if rotated(j, hh):
                     nc.vector.scalar_tensor_tensor(
-                        out=u_t[:], in0=acc[:], scalar=b_t[:, h : h + 1], in1=cos_t[:, cols], op0=ADD, op1=MULT
-                    )
-                    nc.vector.scalar_tensor_tensor(
-                        out=w_t[:], in0=acc[:], scalar=b_t[:, h : h + 1], in1=sin_t[:, cols], op0=ADD, op1=MULT
+                        out=uw[:],
+                        in0=acc[:].unsqueeze(1).to_broadcast([P, 2, HALF]),
+                        scalar=b_t[:, col : col + 1],
+                        in1=tab_t[:, half],
+                        op0=ADD,
+                        op1=MULT,
                     )
                 else:
-                    nc.scalar.activation(out=u_t[:], in_=acc[:], func=ACT.Identity, bias=b_t[:, h : h + 1])
+                    nc.scalar.activation(
+                        out=uw[:, 0, :], in_=acc[:], func=ACT.Identity, bias=b_t[:, col : col + 1]
+                    )
                 for extra in extras[hh]:
                     extra()
 
         def back(r):
-            c, half = divmod(r, 2)
+            j, half = divmod(r, 2)
             for t in range(4):
                 o_ps = bank(t, [P, 512], F32)
                 blk = slice(P * t, P * t + P)
                 for hh in range(4):
                     dst = o_ps[:, P * hh : P * hh + P]
-                    if 4 * c + hh < 14:
+                    uw = uws[r][hh]
+                    if rotated(j, hh):
                         nc.tensor.matmul(
-                            out=dst, lhsT=us[r][hh][:, blk], rhs=ident_f[:], is_transpose=True, start=True, stop=False
+                            out=dst, lhsT=uw[:, 0, blk], rhs=ident_f[:], is_transpose=True, start=True, stop=False
                         )
                         nc.tensor.matmul(
-                            out=dst, lhsT=wss[r][hh][:, blk], rhs=perm_f[:], is_transpose=True, start=False, stop=True
+                            out=dst, lhsT=uw[:, 1, blk], rhs=perm_f[:], is_transpose=True, start=False, stop=True
                         )
                     else:
-                        nc.tensor.transpose(dst, us[r][hh][:, blk], ident_f[:])
+                        nc.tensor.transpose(dst, uw[:, 0, blk], ident_f[:])
                 o_sb = outp.tile([P, 512], F32, name="o_sb", tag="o_sb")
                 nc.scalar.copy(out=o_sb[:], in_=o_ps[:])
                 t8 = 4 * half + t
-                if c < 3:
-                    nc.sync.dma_start(out=o0_v[:, t8, 512 * c : 512 * c + 512], in_=o_sb[:])
-                else:
+                if j == 0:
                     nc.sync.dma_start(out=o1_v[:, t8, :], in_=o_sb[:, 0:256])
                     nc.sync.dma_start(out=o2_v[:, t8, :], in_=o_sb[:, 256:512])
+                else:
+                    nc.sync.dma_start(out=o0_v[:, t8, 512 * (j - 1) : 512 * j], in_=o_sb[:])
 
         x_transposes(0, (0, 1, 2, 3, 4, 5))
         regroup(True, 0, 0)
@@ -265,30 +273,33 @@ def tile_qwen2vlattention_pa_kernel(
         project(0, (0, 1, 2, 3), True)
         bias_transpose(6)
         table_transposes(0, 7)
-        x_transposes(1, (4, 5, 6, 7, 4, 5))
         table_transposes(1, 6)
+        x_transposes(1, (4, 5, 7, 6, 4, 5))
         rope(0, [[], [lambda: quant_x(1, 0)], [lambda: quant_x(1, 1)], [lambda: quant_x(1, 2)]])
         project(1, (4, 5, 6, 7), False)
 
-        s_pre = {
-            0: [(1, 0), (1, 2)],
-            1: [(2, 0), (2, 1)],
-            2: [(2, 2)],
-            3: [(3, 0), (3, 1)],
-            4: [(3, 2)],
-        }
-        v_mix = {
-            0: [[lambda: regroup(True, 1, 1)], [lambda: quant_w(1, 0)], [lambda: quant_w(1, 1)], [lambda: quant_w(1, 2)]],
-            1: [[], [lambda: quant_w(2, 0)], [], [lambda: quant_w(2, 1)]],
-            2: [[lambda: quant_w(2, 2)], [], [], []],
-            3: [[], [lambda: quant_w(3, 0)], [], [lambda: quant_w(3, 1)]],
-            4: [[lambda: quant_w(3, 2)], [], [], []],
-        }
+        def passes_due(r):
+            if r == 0:
+                return [(1, 0), (1, 1), (1, 2)]
+            if r % 2 == 1 and (r + 3) // 2 < 4:
+                return [((r + 3) // 2, 0), ((r + 3) // 2, 1)]
+            if r % 2 == 0 and (r + 2) // 2 < 4:
+                return [((r + 2) // 2, 2)]
+            return []
+
+        def later(fn, j, g):
+            return lambda: fn(j, g)
+
         for r in range(8):
-            for c, g in s_pre.get(r, []):
-                regroup(False, c, g)
+            extras = [[], [], [], []]
+            for k, (j, g) in enumerate(passes_due(r)):
+                if r == 0 and g == 1:
+                    extras[0].append(lambda: regroup(True, 1, 1))
+                else:
+                    regroup(False, j, g)
+                extras[k + 1].append(later(quant_w, j, g))
             back(r)
             if r + 1 < 8:
-                rope(r + 1, v_mix.get(r, [[], [], [], []]))
+                rope(r + 1, extras)
             if r + 2 < 8:
                 project(r + 2, (4, 5, 6, 7), False)

@@ -43,7 +43,7 @@ def tile_qwen2vlattention_pa_kernel(
     with ExitStack() as ctx:
         keep = ctx.enter_context(tc.tile_pool(name="keep", bufs=1))
         xgp = ctx.enter_context(tc.tile_pool(name="xgp", bufs=3))
-        wgp = ctx.enter_context(tc.tile_pool(name="wgp", bufs=4))
+        wgp = ctx.enter_context(tc.tile_pool(name="wgp", bufs=2))
         uwp = ctx.enter_context(tc.tile_pool(name="uwp", bufs=2))
         outp = ctx.enter_context(tc.tile_pool(name="outp", bufs=8))
         psum = ctx.enter_context(tc.psum_pool(name="psum", bufs=1))
@@ -159,17 +159,21 @@ def tile_qwen2vlattention_pa_kernel(
                 out=xq[:, half, g, :].bitcast(FP8X4), scales=xs[:, half, g, :], in_=xg[(half, g)][:]
             )
 
-        def regroup(on_vector, j, g):
-            grouped = wgp.tile([P, 2048], BF16, name="wg", tag="wg", align_bytes=64)
+        def regroup(engine, j, g):
+            grouped = wgp.tile([P, 2048], BF16, name="wg_" + engine, tag="wg_" + engine, align_bytes=64)
             wg[(j, g)] = grouped
             blocks = w_raw[j][g].shape[1]
             dst = grouped[:].rearrange("p (b c i t) -> p b c t i", b=blocks, i=4, t=4)
             src = w_raw[j][g][:].rearrange("p b t (c i) -> p b c t i", i=4)
             for blk in range(blocks):
-                if on_vector:
+                if engine == "vector":
                     nc.vector.tensor_copy(out=dst[:, blk], in_=src[:, blk])
-                else:
+                elif engine == "scalar":
                     nc.scalar.copy(out=dst[:, blk], in_=src[:, blk])
+                else:
+                    nc.gpsimd.tensor_scalar(
+                        out=dst[:, blk], in0=src[:, blk], scalar1=1.0, scalar2=0.0, op0=MULT, op1=ADD
+                    )
 
         def quant_w(j, g):
             nc.vector.quantize_mx(
@@ -261,12 +265,12 @@ def tile_qwen2vlattention_pa_kernel(
                     nc.sync.dma_start(out=o0_v[:, t8, 512 * (j - 1) : 512 * j], in_=o_sb[:])
 
         x_transposes(0, (0, 1, 2, 3, 4, 5))
-        regroup(True, 0, 0)
+        regroup("vector", 0, 0)
         quant_x(0, 0)
-        regroup(True, 0, 1)
+        regroup("vector", 0, 1)
         quant_x(0, 1)
         quant_w(0, 0)
-        regroup(True, 0, 2)
+        regroup("vector", 0, 2)
         quant_x(0, 2)
         quant_w(0, 1)
         quant_w(0, 2)
@@ -278,26 +282,18 @@ def tile_qwen2vlattention_pa_kernel(
         rope(0, [[], [lambda: quant_x(1, 0)], [lambda: quant_x(1, 1)], [lambda: quant_x(1, 2)]])
         project(1, (4, 5, 6, 7), False)
 
-        def passes_due(r):
-            if r == 0:
-                return [(1, 0), (1, 1), (1, 2)]
-            if r % 2 == 1 and (r + 3) // 2 < 4:
-                return [((r + 3) // 2, 0), ((r + 3) // 2, 1)]
-            if r % 2 == 0 and (r + 2) // 2 < 4:
-                return [((r + 2) // 2, 2)]
-            return []
-
-        def later(fn, j, g):
-            return lambda: fn(j, g)
+        def later(fn, a, b, c):
+            return lambda: fn(a, b, c) if a else fn(b, c)
 
         for r in range(8):
             extras = [[], [], [], []]
-            for k, (j, g) in enumerate(passes_due(r)):
-                if r == 0 and g == 1:
-                    extras[0].append(lambda: regroup(True, 1, 1))
-                else:
-                    regroup(False, j, g)
-                extras[k + 1].append(later(quant_w, j, g))
+            for j in range(1, 4):
+                if r == max(0, 2 * j - 3):
+                    regroup("gpsimd", j, 0)
+                    regroup("scalar", j, 1)
+                    extras[0].append(later(regroup, "vector", j, 2))
+                    for g in range(PASSES):
+                        extras[g + 1].append(later(quant_w, None, j, g))
             back(r)
             if r + 1 < 8:
                 rope(r + 1, extras)

@@ -43,7 +43,7 @@ def tile_qwen2vlattention_pa_kernel(
     with ExitStack() as ctx:
         keep = ctx.enter_context(tc.tile_pool(name="keep", bufs=1))
         xgp = ctx.enter_context(tc.tile_pool(name="xgp", bufs=3))
-        wgp = ctx.enter_context(tc.tile_pool(name="wgp", bufs=2))
+        wgp = ctx.enter_context(tc.tile_pool(name="wgp", bufs=4))
         uwp = ctx.enter_context(tc.tile_pool(name="uwp", bufs=2))
         outp = ctx.enter_context(tc.tile_pool(name="outp", bufs=8))
         psum = ctx.enter_context(tc.psum_pool(name="psum", bufs=1))
@@ -159,21 +159,17 @@ def tile_qwen2vlattention_pa_kernel(
                 out=xq[:, half, g, :].bitcast(FP8X4), scales=xs[:, half, g, :], in_=xg[(half, g)][:]
             )
 
-        def regroup(engine, j, g):
-            grouped = wgp.tile([P, 2048], BF16, name="wg_" + engine, tag="wg_" + engine, align_bytes=64)
+        def regroup(on_vector, j, g):
+            grouped = wgp.tile([P, 2048], BF16, name="wg", tag="wg", align_bytes=64)
             wg[(j, g)] = grouped
             blocks = w_raw[j][g].shape[1]
             dst = grouped[:].rearrange("p (b c i t) -> p b c t i", b=blocks, i=4, t=4)
             src = w_raw[j][g][:].rearrange("p b t (c i) -> p b c t i", i=4)
             for blk in range(blocks):
-                if engine == "vector":
+                if on_vector:
                     nc.vector.tensor_copy(out=dst[:, blk], in_=src[:, blk])
-                elif engine == "scalar":
-                    nc.scalar.copy(out=dst[:, blk], in_=src[:, blk])
                 else:
-                    nc.gpsimd.tensor_scalar(
-                        out=dst[:, blk], in0=src[:, blk], scalar1=1.0, scalar2=0.0, op0=MULT, op1=ADD
-                    )
+                    nc.scalar.copy(out=dst[:, blk], in_=src[:, blk])
 
         def quant_w(j, g):
             nc.vector.quantize_mx(
@@ -240,37 +236,43 @@ def tile_qwen2vlattention_pa_kernel(
 
         def back(r):
             j, half = divmod(r, 2)
-            for t in range(4):
-                o_ps = bank(t, [P, 512], F32)
-                blk = slice(P * t, P * t + P)
+            for tp in range(2):
+                pair = (2 * tp, 2 * tp + 1)
+                o_ps = [bank(t, [P, 512], F32) for t in pair]
                 for hh in range(4):
-                    dst = o_ps[:, P * hh : P * hh + P]
                     uw = uws[r][hh]
+                    cols = slice(P * hh, P * hh + P)
                     if rotated(j, hh):
-                        nc.tensor.matmul(
-                            out=dst, lhsT=uw[:, 0, blk], rhs=ident_f[:], is_transpose=True, start=True, stop=False
-                        )
-                        nc.tensor.matmul(
-                            out=dst, lhsT=uw[:, 1, blk], rhs=perm_f[:], is_transpose=True, start=False, stop=True
-                        )
+                        for o_t, t in zip(o_ps, pair):
+                            nc.tensor.matmul(
+                                out=o_t[:, cols], lhsT=uw[:, 0, P * t : P * t + P], rhs=ident_f[:],
+                                is_transpose=True, start=True, stop=False,
+                            )
+                        for o_t, t in zip(o_ps, pair):
+                            nc.tensor.matmul(
+                                out=o_t[:, cols], lhsT=uw[:, 1, P * t : P * t + P], rhs=perm_f[:],
+                                is_transpose=True, start=False, stop=True,
+                            )
                     else:
-                        nc.tensor.transpose(dst, uw[:, 0, blk], ident_f[:])
-                o_sb = outp.tile([P, 512], F32, name="o_sb", tag="o_sb")
-                nc.scalar.copy(out=o_sb[:], in_=o_ps[:])
-                t8 = 4 * half + t
-                if j == 0:
-                    nc.sync.dma_start(out=o1_v[:, t8, :], in_=o_sb[:, 0:256])
-                    nc.sync.dma_start(out=o2_v[:, t8, :], in_=o_sb[:, 256:512])
-                else:
-                    nc.sync.dma_start(out=o0_v[:, t8, 512 * (j - 1) : 512 * j], in_=o_sb[:])
+                        for o_t, t in zip(o_ps, pair):
+                            nc.tensor.transpose(o_t[:, cols], uw[:, 0, P * t : P * t + P], ident_f[:])
+                for o_t, t in zip(o_ps, pair):
+                    o_sb = outp.tile([P, 512], F32, name="o_sb", tag="o_sb")
+                    nc.scalar.copy(out=o_sb[:], in_=o_t[:])
+                    t8 = 4 * half + t
+                    if j == 0:
+                        nc.sync.dma_start(out=o1_v[:, t8, :], in_=o_sb[:, 0:256])
+                        nc.sync.dma_start(out=o2_v[:, t8, :], in_=o_sb[:, 256:512])
+                    else:
+                        nc.sync.dma_start(out=o0_v[:, t8, 512 * (j - 1) : 512 * j], in_=o_sb[:])
 
         x_transposes(0, (0, 1, 2, 3, 4, 5))
-        regroup("vector", 0, 0)
+        regroup(True, 0, 0)
         quant_x(0, 0)
-        regroup("vector", 0, 1)
+        regroup(True, 0, 1)
         quant_x(0, 1)
         quant_w(0, 0)
-        regroup("vector", 0, 2)
+        regroup(True, 0, 2)
         quant_x(0, 2)
         quant_w(0, 1)
         quant_w(0, 2)
@@ -282,18 +284,26 @@ def tile_qwen2vlattention_pa_kernel(
         rope(0, [[], [lambda: quant_x(1, 0)], [lambda: quant_x(1, 1)], [lambda: quant_x(1, 2)]])
         project(1, (4, 5, 6, 7), False)
 
-        def later(fn, a, b, c):
-            return lambda: fn(a, b, c) if a else fn(b, c)
+        def passes_due(r):
+            if r == 0:
+                return [(1, 0), (1, 1), (1, 2)]
+            if r % 2 == 1 and (r + 3) // 2 < 4:
+                return [((r + 3) // 2, 0), ((r + 3) // 2, 1)]
+            if r % 2 == 0 and (r + 2) // 2 < 4:
+                return [((r + 2) // 2, 2)]
+            return []
+
+        def later(fn, j, g):
+            return lambda: fn(j, g)
 
         for r in range(8):
             extras = [[], [], [], []]
-            for j in range(1, 4):
-                if r == max(0, 2 * j - 3):
-                    regroup("gpsimd", j, 0)
-                    regroup("scalar", j, 1)
-                    extras[0].append(later(regroup, "vector", j, 2))
-                    for g in range(PASSES):
-                        extras[g + 1].append(later(quant_w, None, j, g))
+            for k, (j, g) in enumerate(passes_due(r)):
+                if r == 0 and g == 1:
+                    extras[0].append(lambda: regroup(True, 1, 1))
+                else:
+                    regroup(False, j, g)
+                extras[k + 1].append(later(quant_w, j, g))
             back(r)
             if r + 1 < 8:
                 rope(r + 1, extras)

@@ -15,297 +15,298 @@ ACT = mybir.ActivationFunctionType
 P = 128
 S = 1024
 M = 1536
-PASSES = 3
-T8 = 8
-HALF = 512
+PACK = 4
+PASSES = M // (P * PACK)
+TILES = S // P
+HALF = S // 2
+HALF_TILES = TILES // 2
+CHUNKS = 4
+CHUNK_HEADS = 4
+CHUNK = CHUNK_HEADS * P
+ROUNDS = 2 * CHUNKS
+HEADS = CHUNKS * CHUNK_HEADS
 
-FLOPS = 2 * S * M * 2048
-BYTES = S * M * 2 + M * 2048 * 2 + 16 * 128 * 2 + 2 * S * 128 * 2 + S * 2048 * 4
+FLOPS = 2 * S * M * HEADS * P
+BYTES = S * M * 2 + M * HEADS * P * 2 + HEADS * P * 2 + 2 * S * P * 2 + S * HEADS * P * 4
 
-COS_PARTS = ((0, 0, 32, 0), (1, 32, 80, 32), (2, 80, 128, 80))
-SIN_PARTS = ((1, 64, 80, 0), (2, 80, 128, 16), (0, 0, 32, 64), (1, 32, 64, 96))
+COS_SECTIONS = ((0, 0, 32, 0), (1, 32, 80, 32), (2, 80, 128, 80))
+SIN_SECTIONS = ((1, 64, 80, 0), (2, 80, 128, 16), (0, 0, 32, 64), (1, 32, 64, 96))
+
+LOW_BANKS = (0, 1, 2, 3)
+HIGH_BANKS = (4, 5, 6, 7)
+X_BANKS = ((0, 1, 2, 3, 4, 5), (4, 5, 6, 7, 4, 5))
+BIAS_BANK = 6
+TABLE_BANKS = (7, 6)
+
+NOTHING_BETWEEN = ((), (), (), ())
 
 
 def tile_qwen2vlattention_pa_kernel(
     tc, hidden_states, cos, sin, Wq, bq, Wk, bk, Wv, bv, out_0, out_1, out_2
 ):
     nc = tc.nc
-    x_v = hidden_states.rearrange("b s m -> (b s) m").rearrange("(p t) m -> p t m", t=T8)
-    cos_v = cos.rearrange("c b s d -> c (b s) d")
-    sin_v = sin.rearrange("c b s d -> c (b s) d")
-    wq_v = Wq.rearrange("m h d -> m (h d)")
-    wk_v = Wk.rearrange("m h d -> m (h d)")
-    wv_v = Wv.rearrange("m h d -> m (h d)")
-    o0_v = out_0.rearrange("b s h d -> (b s) (h d)").rearrange("(p t) n -> p t n", t=T8)
-    o1_v = out_1.rearrange("b s h d -> (b s) (h d)").rearrange("(p t) n -> p t n", t=T8)
-    o2_v = out_2.rearrange("b s h d -> (b s) (h d)").rearrange("(p t) n -> p t n", t=T8)
+    x_dram = hidden_states.rearrange("b s m -> (b s) m").rearrange("(p t) m -> p t m", t=TILES)
+    cos_dram = cos.rearrange("c b s d -> c (b s) d")
+    sin_dram = sin.rearrange("c b s d -> c (b s) d")
+    wq_dram = Wq.rearrange("m h d -> m (h d)")
+    wk_dram = Wk.rearrange("m h d -> m (h d)")
+    wv_dram = Wv.rearrange("m h d -> m (h d)")
+    q_dram = out_0.rearrange("b s h d -> (b s) (h d)").rearrange("(p t) n -> p t n", t=TILES)
+    k_dram = out_1.rearrange("b s h d -> (b s) (h d)").rearrange("(p t) n -> p t n", t=TILES)
+    v_dram = out_2.rearrange("b s h d -> (b s) (h d)").rearrange("(p t) n -> p t n", t=TILES)
 
     with ExitStack() as ctx:
         keep = ctx.enter_context(tc.tile_pool(name="keep", bufs=1))
-        xgp = ctx.enter_context(tc.tile_pool(name="xgp", bufs=3))
-        wgp = ctx.enter_context(tc.tile_pool(name="wgp", bufs=4))
-        uwp = ctx.enter_context(tc.tile_pool(name="uwp", bufs=2))
-        outp = ctx.enter_context(tc.tile_pool(name="outp", bufs=8))
+        x_grouped_pool = ctx.enter_context(tc.tile_pool(name="x_grouped", bufs=PASSES))
+        w_grouped_pool = ctx.enter_context(tc.tile_pool(name="w_grouped", bufs=PASSES + 1))
+        uw_pool = ctx.enter_context(tc.tile_pool(name="uw", bufs=2))
+        out_pool = ctx.enter_context(tc.tile_pool(name="out", bufs=2 * HALF_TILES))
         psum = ctx.enter_context(tc.psum_pool(name="psum", bufs=1))
         ctx.enter_context(tc.manual_schedule())
 
         def bank(i, shape, dtype):
             return psum.tile(shape, dtype, name="bank%d" % i, tag="bank%d" % i)
 
-        ident_f = keep.tile([P, P], F32, name="ident_f")
-        ident_b = keep.tile([P, P], BF16, name="ident_b")
-        perm_f = keep.tile([P, P], F32, name="perm_f")
-        sgn = keep.tile([P, 1], F32, name="sgn")
-        b_raw = keep.tile([P, P], BF16, name="b_raw")
-        b_t = keep.tile([P, 16], F32, name="b_t")
-        c_raw = keep.tile([P, T8, P], BF16, name="c_raw")
-        s_raw = keep.tile([P, T8, P], BF16, name="s_raw")
-        tab_t = keep.tile([P, 2, 2, HALF], BF16, name="tab_t")
-        x_raw = keep.tile([P, T8 * M], BF16, name="x_raw")
-        xq = keep.tile([P, 2, PASSES, HALF], U32, name="xq", align_bytes=64)
-        xs = keep.tile([P, 2, PASSES, HALF], U8, name="xs", align_bytes=64)
-        wq = [keep.tile([P, PASSES, 512], U32, name="wq%d" % j, align_bytes=64) for j in range(4)]
-        ws = [keep.tile([P, PASSES, 512], U8, name="ws%d" % j, align_bytes=64) for j in range(4)]
-        w_raw = [
-            [keep.tile([P, 2, 4, 256], BF16, name="wraw%d_%d" % (j, g)) for g in range(PASSES)]
-            if j == 0
-            else [keep.tile([P, 1, 4, 512], BF16, name="wraw%d_%d" % (j, g)) for g in range(PASSES)]
-            for j in range(4)
-        ]
-        x_w = x_raw[:].bitcast(F32)
+        identity_f32 = keep.tile([P, P], F32, name="identity_f32")
+        identity_bf16 = keep.tile([P, P], BF16, name="identity_bf16")
+        swap_halves = keep.tile([P, P], F32, name="swap_halves")
+        sin_sign = keep.tile([P, 1], F32, name="sin_sign")
+        bias_rows = keep.tile([P, P], BF16, name="bias_rows")
+        bias_t = keep.tile([P, HEADS], F32, name="bias_t")
+        cos_rows = keep.tile([P, TILES, P], BF16, name="cos_rows")
+        sin_rows = keep.tile([P, TILES, P], BF16, name="sin_rows")
+        tables_t = keep.tile([P, 2, 2, HALF], BF16, name="tables_t")
+        x_rows = keep.tile([P, TILES * M], BF16, name="x_rows")
+        x_codes = keep.tile([P, 2, PASSES, HALF], U32, name="x_codes", align_bytes=64)
+        x_scales = keep.tile([P, 2, PASSES, HALF], U8, name="x_scales", align_bytes=64)
+        w_codes = [keep.tile([P, PASSES, CHUNK], U32, name="w_codes%d" % j, align_bytes=64) for j in range(CHUNKS)]
+        w_scales = [keep.tile([P, PASSES, CHUNK], U8, name="w_scales%d" % j, align_bytes=64) for j in range(CHUNKS)]
 
-        make_identity(nc, ident_f[:])
-        make_identity(nc, ident_b[:])
-        nc.vector.memset(b_raw[:], 0.0)
-        nc.vector.memset(sgn[0:64, :], 1.0)
-        nc.vector.memset(sgn[64:128, :], -1.0)
-        nc.vector.tensor_copy(out=perm_f[:, 0:64], in_=ident_f[:, 64:128])
-        nc.vector.tensor_copy(out=perm_f[:, 64:128], in_=ident_f[:, 0:64])
+        def weight_sources(j):
+            if j == 0:
+                return (wk_dram, wv_dram)
+            return (wq_dram[:, CHUNK * (j - 1) : CHUNK * j],)
+
+        w_rows = [
+            [
+                keep.tile(
+                    [P, len(weight_sources(j)), PACK, CHUNK // len(weight_sources(j))],
+                    BF16,
+                    name="w_rows%d_%d" % (j, g),
+                )
+                for g in range(PASSES)
+            ]
+            for j in range(CHUNKS)
+        ]
+
+        make_identity(nc, identity_f32[:])
+        make_identity(nc, identity_bf16[:])
+        nc.vector.memset(bias_rows[:], 0.0)
+        nc.vector.memset(sin_sign[0 : P // 2, :], 1.0)
+        nc.vector.memset(sin_sign[P // 2 : P, :], -1.0)
+        nc.vector.tensor_copy(out=swap_halves[:, 0 : P // 2], in_=identity_f32[:, P // 2 : P])
+        nc.vector.tensor_copy(out=swap_halves[:, P // 2 : P], in_=identity_f32[:, 0 : P // 2])
 
         def load_x(half):
-            for tp in range(2):
-                t8 = 4 * half + 2 * tp
+            for t in range(HALF_TILES * half, HALF_TILES * (half + 1), 2):
                 nc.sync.dma_start(
-                    out=x_raw[:, t8 * M : (t8 + 2) * M],
-                    in_=x_v[:, t8 : t8 + 2, :].rearrange("p t m -> p (t m)"),
+                    out=x_rows[:, t * M : (t + 2) * M],
+                    in_=x_dram[:, t : t + 2, :].rearrange("p t m -> p (t m)"),
                 )
 
-        def load_w(j):
+        def load_weights(j):
             for g in range(PASSES):
                 for u in range(2):
-                    rows = slice(512 * g + 256 * u, 512 * g + 256 * u + 256)
-                    if j == 0:
-                        sources = (wk_v[rows, :], wv_v[rows, :])
-                    else:
-                        sources = (wq_v[rows, 512 * (j - 1) : 512 * j],)
-                    for blk, src in enumerate(sources):
+                    first = P * PACK * g + 2 * P * u
+                    for n, source in enumerate(weight_sources(j)):
                         nc.sync.dma_start(
-                            out=w_raw[j][g][:, blk, 2 * u : 2 * u + 2, :],
-                            in_=src.rearrange("(q e) n -> q e n", e=2),
+                            out=w_rows[j][g][:, n, 2 * u : 2 * u + 2, :],
+                            in_=source[first : first + 2 * P, :].rearrange("(p e) c -> p e c", e=2),
                         )
 
         def load_tables(half):
-            ts = slice(4 * half, 4 * half + 4)
-            for comp, lo, hi, dlo in COS_PARTS:
-                src = cos_v[comp].rearrange("(p t) d -> p t d", t=T8)
-                nc.sync.dma_start(out=c_raw[:, ts, dlo : dlo + hi - lo], in_=src[:, ts, lo:hi])
-            for comp, lo, hi, dlo in SIN_PARTS:
-                src = sin_v[comp].rearrange("(p t) d -> p t d", t=T8)
-                nc.sync.dma_start(out=s_raw[:, ts, dlo : dlo + hi - lo], in_=src[:, ts, lo:hi])
+            tiles = slice(HALF_TILES * half, HALF_TILES * (half + 1))
+            for rows, dram, sections in ((cos_rows, cos_dram, COS_SECTIONS), (sin_rows, sin_dram, SIN_SECTIONS)):
+                for component, lo, hi, column in sections:
+                    source = dram[component].rearrange("(p t) d -> p t d", t=TILES)
+                    nc.sync.dma_start(out=rows[:, tiles, column : column + hi - lo], in_=source[:, tiles, lo:hi])
 
         load_x(0)
-        load_w(0)
-        nc.sync.dma_start(out=b_raw[0:12, :], in_=bq)
-        nc.sync.dma_start(out=b_raw[12:14, :], in_=bk)
-        nc.sync.dma_start(out=b_raw[14:16, :], in_=bv)
+        load_weights(0)
+        nc.sync.dma_start(out=bias_rows[0:12, :], in_=bq)
+        nc.sync.dma_start(out=bias_rows[12:14, :], in_=bk)
+        nc.sync.dma_start(out=bias_rows[14:16, :], in_=bv)
         load_tables(0)
         load_tables(1)
         load_x(1)
-        load_w(1)
-        load_w(2)
-        load_w(3)
+        for j in range(1, CHUNKS):
+            load_weights(j)
 
-        xg = {}
-        wg = {}
-        accs = {}
-        uws = {}
+        x_grouped = {}
+        w_grouped = {}
+        sums = {}
+        products = {}
 
-        def bias_column(j, hh):
-            return 12 + hh if j == 0 else 4 * (j - 1) + hh
+        def bias_column(j, head):
+            return 12 + head if j == 0 else CHUNK_HEADS * (j - 1) + head
 
-        def rotated(j, hh):
-            return j > 0 or hh < 2
+        def is_rotated(j, head):
+            return j > 0 or head < 2
 
-        def x_transposes(half, banks):
-            words = []
+        def transpose_x(half):
+            x_words = x_rows[:].bitcast(F32)
+            grouped_words = []
             for g in range(PASSES):
-                grouped = xgp.tile([P, 2048], BF16, name="xg", tag="xg", align_bytes=64)
-                xg[(half, g)] = grouped
-                words.append(grouped[:].bitcast(F32).rearrange("p (tt s u) -> p tt s u", tt=4, u=2))
-            for tp in range(2):
+                grouped = x_grouped_pool.tile([P, PACK * HALF], BF16, name="x_grouped", tag="x_grouped", align_bytes=64)
+                x_grouped[(half, g)] = grouped
+                grouped_words.append(
+                    grouped[:].bitcast(F32).rearrange("p (t s u) -> p t s u", t=HALF_TILES, u=2)
+                )
+            for pair in range(HALF_TILES // 2):
                 for g in range(PASSES):
-                    xt = bank(banks[PASSES * tp + g], [P, 2, 2, P], F32)
-                    for tt in range(2):
+                    turned = bank(X_BANKS[half][PASSES * pair + g], [P, 2, 2, P], F32)
+                    for t in range(2):
                         for u in range(2):
-                            col = (4 * half + 2 * tp + tt) * (M // 2) + 256 * g + 128 * u
-                            nc.tensor.transpose(xt[:, tt, u, :], x_w[:, col : col + P], ident_f[:])
+                            column = (HALF_TILES * half + 2 * pair + t) * (M // 2) + 2 * P * g + P * u
+                            nc.tensor.transpose(turned[:, t, u, :], x_words[:, column : column + P], identity_f32[:])
                     nc.scalar.copy(
-                        out=words[g][:, 2 * tp : 2 * tp + 2],
-                        in_=xt[:].rearrange("p tt u s -> p tt s u"),
+                        out=grouped_words[g][:, 2 * pair : 2 * pair + 2],
+                        in_=turned[:].rearrange("p t u s -> p t s u"),
                     )
 
-        def quant_x(half, g):
+        def quantise_x(half, g):
             nc.vector.quantize_mx(
-                out=xq[:, half, g, :].bitcast(FP8X4), scales=xs[:, half, g, :], in_=xg[(half, g)][:]
+                out=x_codes[:, half, g, :].bitcast(FP8X4), scales=x_scales[:, half, g, :], in_=x_grouped[(half, g)][:]
             )
 
-        def regroup(on_vector, j, g):
-            grouped = wgp.tile([P, 2048], BF16, name="wg", tag="wg", align_bytes=64)
-            wg[(j, g)] = grouped
-            blocks = w_raw[j][g].shape[1]
-            dst = grouped[:].rearrange("p (b c i t) -> p b c t i", b=blocks, i=4, t=4)
-            src = w_raw[j][g][:].rearrange("p b t (c i) -> p b c t i", i=4)
-            for blk in range(blocks):
-                if on_vector:
-                    nc.vector.tensor_copy(out=dst[:, blk], in_=src[:, blk])
-                else:
-                    nc.scalar.copy(out=dst[:, blk], in_=src[:, blk])
+        def regroup_weights(copy, j, g):
+            grouped = w_grouped_pool.tile([P, PACK * CHUNK], BF16, name="w_grouped", tag="w_grouped", align_bytes=64)
+            w_grouped[(j, g)] = grouped
+            sources = len(weight_sources(j))
+            target = grouped[:].rearrange("p (n c i v) -> p n c v i", n=sources, i=4, v=PACK)
+            rows = w_rows[j][g][:].rearrange("p n v (c i) -> p n c v i", i=4)
+            for n in range(sources):
+                copy(out=target[:, n], in_=rows[:, n])
 
-        def quant_w(j, g):
+        def quantise_weights(j, g):
             nc.vector.quantize_mx(
-                out=wq[j][:, g, :].bitcast(FP8X4), scales=ws[j][:, g, :], in_=wg[(j, g)][:]
+                out=w_codes[j][:, g, :].bitcast(FP8X4), scales=w_scales[j][:, g, :], in_=w_grouped[(j, g)][:]
             )
 
         def project(r, banks, pass_outer):
             j, half = divmod(r, 2)
-            tiles = [bank(b, [P, HALF], F32) for b in banks]
-            accs[r] = tiles
+            sums[r] = [bank(b, [P, HALF], F32) for b in banks]
             if pass_outer:
-                order = [(g, hh) for g in range(PASSES) for hh in range(4)]
+                order = [(g, head) for g in range(PASSES) for head in range(CHUNK_HEADS)]
             else:
-                order = [(g, hh) for hh in range(4) for g in range(PASSES)]
-            for g, hh in order:
-                cols = slice(P * hh, P * hh + P)
+                order = [(g, head) for head in range(CHUNK_HEADS) for g in range(PASSES)]
+            for g, head in order:
+                columns = slice(P * head, P * (head + 1))
                 nc.tensor.matmul_mx(
-                    out=tiles[hh][:],
-                    lhsT=wq[j][:, g, cols].bitcast(FP8X4),
-                    lhsT_scale=ws[j][:, g, cols],
-                    rhs=xq[:, half, g, :].bitcast(FP8X4),
-                    rhs_scale=xs[:, half, g, :],
+                    out=sums[r][head][:],
+                    lhsT=w_codes[j][:, g, columns].bitcast(FP8X4),
+                    lhsT_scale=w_scales[j][:, g, columns],
+                    rhs=x_codes[:, half, g, :].bitcast(FP8X4),
+                    rhs_scale=x_scales[:, half, g, :],
                     start=(g == 0),
                     stop=(g == PASSES - 1),
                 )
 
-        def bias_transpose(b):
-            bt = bank(b, [P, P], BF16)
-            nc.tensor.transpose(bt[:], b_raw[:], ident_b[:])
-            nc.vector.tensor_copy(out=b_t[:], in_=bt[:, 0:16])
+        def transpose_biases():
+            turned = bank(BIAS_BANK, [P, P], BF16)
+            nc.tensor.transpose(turned[:], bias_rows[:], identity_bf16[:])
+            nc.vector.tensor_copy(out=bias_t[:], in_=turned[:, 0:HEADS])
 
-        def table_transposes(half, b):
-            tb = bank(b, [P, 2, HALF], BF16)
-            for t in range(4):
-                nc.tensor.transpose(tb[:, 0, P * t : P * t + P], c_raw[:, 4 * half + t, :], ident_b[:])
-            for t in range(4):
-                nc.tensor.transpose(tb[:, 1, P * t : P * t + P], s_raw[:, 4 * half + t, :], ident_b[:])
-            nc.scalar.copy(out=tab_t[:, half, 0, :], in_=tb[:, 0, :])
-            nc.scalar.activation(out=tab_t[:, half, 1, :], in_=tb[:, 1, :], func=ACT.Copy, scale=sgn[:, 0:1])
+        def transpose_tables(half):
+            turned = bank(TABLE_BANKS[half], [P, 2, HALF], BF16)
+            for table, rows in enumerate((cos_rows, sin_rows)):
+                for t in range(HALF_TILES):
+                    nc.tensor.transpose(
+                        turned[:, table, P * t : P * (t + 1)], rows[:, HALF_TILES * half + t, :], identity_bf16[:]
+                    )
+            nc.scalar.copy(out=tables_t[:, half, 0, :], in_=turned[:, 0, :])
+            nc.scalar.activation(out=tables_t[:, half, 1, :], in_=turned[:, 1, :], func=ACT.Copy, scale=sin_sign[:, 0:1])
 
-        def rope(r, extras):
+        def add_bias_and_multiply(r, between):
             j, half = divmod(r, 2)
-            uws[r] = []
-            for hh in range(4):
-                col = bias_column(j, hh)
-                acc = accs[r][hh]
-                uw = uwp.tile([P, 2, HALF], F32, name="uw%d" % hh, tag="uw%d" % hh)
-                uws[r].append(uw)
-                if rotated(j, hh):
+            products[r] = []
+            for head in range(CHUNK_HEADS):
+                bias = bias_t[:, bias_column(j, head) : bias_column(j, head) + 1]
+                uw = uw_pool.tile([P, 2, HALF], F32, name="uw%d" % head, tag="uw%d" % head)
+                products[r].append(uw)
+                if is_rotated(j, head):
                     nc.vector.scalar_tensor_tensor(
                         out=uw[:],
-                        in0=acc[:].unsqueeze(1).to_broadcast([P, 2, HALF]),
-                        scalar=b_t[:, col : col + 1],
-                        in1=tab_t[:, half],
+                        in0=sums[r][head][:].unsqueeze(1).to_broadcast([P, 2, HALF]),
+                        scalar=bias,
+                        in1=tables_t[:, half],
                         op0=ADD,
                         op1=MULT,
                     )
                 else:
-                    nc.scalar.activation(
-                        out=uw[:, 0, :], in_=acc[:], func=ACT.Identity, bias=b_t[:, col : col + 1]
-                    )
-                for extra in extras[hh]:
-                    extra()
+                    nc.scalar.activation(out=uw[:, 0, :], in_=sums[r][head][:], func=ACT.Identity, bias=bias)
+                for stage, a, b in between[head]:
+                    stage(a, b)
 
-        def back(r):
+        def turn_back_and_store(r):
             j, half = divmod(r, 2)
-            for tp in range(2):
-                pair = (2 * tp, 2 * tp + 1)
-                o_ps = [bank(t, [P, 512], F32) for t in pair]
-                for hh in range(4):
-                    uw = uws[r][hh]
-                    cols = slice(P * hh, P * hh + P)
-                    if rotated(j, hh):
-                        for o_t, t in zip(o_ps, pair):
-                            nc.tensor.matmul(
-                                out=o_t[:, cols], lhsT=uw[:, 0, P * t : P * t + P], rhs=ident_f[:],
-                                is_transpose=True, start=True, stop=False,
-                            )
-                        for o_t, t in zip(o_ps, pair):
-                            nc.tensor.matmul(
-                                out=o_t[:, cols], lhsT=uw[:, 1, P * t : P * t + P], rhs=perm_f[:],
-                                is_transpose=True, start=False, stop=True,
-                            )
+            for t in range(HALF_TILES):
+                result = bank(LOW_BANKS[t], [P, CHUNK], F32)
+                rows = slice(P * t, P * (t + 1))
+                for head in range(CHUNK_HEADS):
+                    target = result[:, P * head : P * (head + 1)]
+                    uw = products[r][head]
+                    if is_rotated(j, head):
+                        nc.tensor.matmul(
+                            out=target, lhsT=uw[:, 0, rows], rhs=identity_f32[:], is_transpose=True, start=True, stop=False
+                        )
+                        nc.tensor.matmul(
+                            out=target, lhsT=uw[:, 1, rows], rhs=swap_halves[:], is_transpose=True, start=False, stop=True
+                        )
                     else:
-                        for o_t, t in zip(o_ps, pair):
-                            nc.tensor.transpose(o_t[:, cols], uw[:, 0, P * t : P * t + P], ident_f[:])
-                for o_t, t in zip(o_ps, pair):
-                    o_sb = outp.tile([P, 512], F32, name="o_sb", tag="o_sb")
-                    nc.scalar.copy(out=o_sb[:], in_=o_t[:])
-                    t8 = 4 * half + t
-                    if j == 0:
-                        nc.sync.dma_start(out=o1_v[:, t8, :], in_=o_sb[:, 0:256])
-                        nc.sync.dma_start(out=o2_v[:, t8, :], in_=o_sb[:, 256:512])
-                    else:
-                        nc.sync.dma_start(out=o0_v[:, t8, 512 * (j - 1) : 512 * j], in_=o_sb[:])
-
-        x_transposes(0, (0, 1, 2, 3, 4, 5))
-        regroup(True, 0, 0)
-        quant_x(0, 0)
-        regroup(True, 0, 1)
-        quant_x(0, 1)
-        quant_w(0, 0)
-        regroup(True, 0, 2)
-        quant_x(0, 2)
-        quant_w(0, 1)
-        quant_w(0, 2)
-        project(0, (0, 1, 2, 3), True)
-        bias_transpose(6)
-        table_transposes(0, 7)
-        table_transposes(1, 6)
-        x_transposes(1, (4, 5, 7, 6, 4, 5))
-        rope(0, [[], [lambda: quant_x(1, 0)], [lambda: quant_x(1, 1)], [lambda: quant_x(1, 2)]])
-        project(1, (4, 5, 6, 7), False)
-
-        def passes_due(r):
-            if r == 0:
-                return [(1, 0), (1, 1), (1, 2)]
-            if r % 2 == 1 and (r + 3) // 2 < 4:
-                return [((r + 3) // 2, 0), ((r + 3) // 2, 1)]
-            if r % 2 == 0 and (r + 2) // 2 < 4:
-                return [((r + 2) // 2, 2)]
-            return []
-
-        def later(fn, j, g):
-            return lambda: fn(j, g)
-
-        for r in range(8):
-            extras = [[], [], [], []]
-            for k, (j, g) in enumerate(passes_due(r)):
-                if r == 0 and g == 1:
-                    extras[0].append(lambda: regroup(True, 1, 1))
+                        nc.tensor.transpose(target, uw[:, 0, rows], identity_f32[:])
+                leaving = out_pool.tile([P, CHUNK], F32, name="leaving", tag="leaving")
+                nc.scalar.copy(out=leaving[:], in_=result[:])
+                tile = HALF_TILES * half + t
+                if j == 0:
+                    nc.sync.dma_start(out=k_dram[:, tile, :], in_=leaving[:, 0 : CHUNK // 2])
+                    nc.sync.dma_start(out=v_dram[:, tile, :], in_=leaving[:, CHUNK // 2 : CHUNK])
                 else:
-                    regroup(False, j, g)
-                extras[k + 1].append(later(quant_w, j, g))
-            back(r)
-            if r + 1 < 8:
-                rope(r + 1, extras)
-            if r + 2 < 8:
-                project(r + 2, (4, 5, 6, 7), False)
+                    nc.sync.dma_start(out=q_dram[:, tile, CHUNK * (j - 1) : CHUNK * j], in_=leaving[:])
+
+        def regroup_on_vector(j, g):
+            regroup_weights(nc.vector.tensor_copy, j, g)
+
+        transpose_x(0)
+        for g in range(PASSES):
+            regroup_on_vector(0, g)
+            quantise_x(0, g)
+            if g > 0:
+                quantise_weights(0, g - 1)
+        quantise_weights(0, PASSES - 1)
+        project(0, LOW_BANKS, True)
+        transpose_biases()
+        transpose_tables(0)
+        transpose_tables(1)
+        add_bias_and_multiply(0, NOTHING_BETWEEN)
+        transpose_x(1)
+        for g in range(PASSES):
+            quantise_x(1, g)
+        project(1, HIGH_BANKS, False)
+
+        for r in range(ROUNDS):
+            due = [
+                (j, g) for j in range(1, CHUNKS) for g in range(PASSES) if r == max(0, 2 * j - 3 + g // 2)
+            ]
+            between = [[] for head in range(CHUNK_HEADS)]
+            for n, (j, g) in enumerate(due):
+                if len(due) == PASSES and n == 1:
+                    between[0].append((regroup_on_vector, j, g))
+                else:
+                    regroup_weights(nc.scalar.copy, j, g)
+                between[n + 1].append((quantise_weights, j, g))
+            turn_back_and_store(r)
+            if r + 1 < ROUNDS:
+                add_bias_and_multiply(r + 1, between)
+            if r + 2 < ROUNDS:
+                project(r + 2, HIGH_BANKS, False)

from contextlib import ExitStack

import concourse.mybir as mybir
from concourse.masks import make_identity

F32 = mybir.dt.float32
BF16 = mybir.dt.bfloat16
U32 = mybir.dt.uint32
U8 = mybir.dt.uint8
FP8X4 = mybir.dt.float8_e4m3fn_x4
ADD = mybir.AluOpType.add
MULT = mybir.AluOpType.mult
ACT = mybir.ActivationFunctionType

P = 128
S = 1024
M = 1536
PACK = 4
PASSES = M // (P * PACK)
TILES = S // P
HALF = S // 2
HALF_TILES = TILES // 2
CHUNKS = 4
CHUNK_HEADS = 4
CHUNK = CHUNK_HEADS * P
ROUNDS = 2 * CHUNKS
HEADS = CHUNKS * CHUNK_HEADS

FLOPS = 2 * S * M * HEADS * P
BYTES = S * M * 2 + M * HEADS * P * 2 + HEADS * P * 2 + 2 * S * P * 2 + S * HEADS * P * 4

COS_SECTIONS = ((0, 0, 32, 0), (1, 32, 80, 32), (2, 80, 128, 80))
SIN_SECTIONS = ((1, 64, 80, 0), (2, 80, 128, 16), (0, 0, 32, 64), (1, 32, 64, 96))

LOW_BANKS = (0, 1, 2, 3)
HIGH_BANKS = (4, 5, 6, 7)
X_BANKS = ((0, 1, 2, 3, 4, 5), (4, 5, 6, 7, 4, 5))
BIAS_BANK = 6
TABLE_BANKS = (7, 6)

NOTHING_BETWEEN = ((), (), (), ())


def tile_qwen2vlattention_pa_kernel(
    tc, hidden_states, cos, sin, Wq, bq, Wk, bk, Wv, bv, out_0, out_1, out_2
):
    nc = tc.nc
    x_dram = hidden_states.rearrange("b s m -> (b s) m").rearrange("(p t) m -> p t m", t=TILES)
    cos_dram = cos.rearrange("c b s d -> c (b s) d")
    sin_dram = sin.rearrange("c b s d -> c (b s) d")
    wq_dram = Wq.rearrange("m h d -> m (h d)")
    wk_dram = Wk.rearrange("m h d -> m (h d)")
    wv_dram = Wv.rearrange("m h d -> m (h d)")
    q_dram = out_0.rearrange("b s h d -> (b s) (h d)").rearrange("(p t) n -> p t n", t=TILES)
    k_dram = out_1.rearrange("b s h d -> (b s) (h d)").rearrange("(p t) n -> p t n", t=TILES)
    v_dram = out_2.rearrange("b s h d -> (b s) (h d)").rearrange("(p t) n -> p t n", t=TILES)

    with ExitStack() as ctx:
        keep = ctx.enter_context(tc.tile_pool(name="keep", bufs=1))
        x_grouped_pool = ctx.enter_context(tc.tile_pool(name="x_grouped", bufs=PASSES))
        w_grouped_pool = ctx.enter_context(tc.tile_pool(name="w_grouped", bufs=PASSES + 1))
        uw_pool = ctx.enter_context(tc.tile_pool(name="uw", bufs=2))
        out_pool = ctx.enter_context(tc.tile_pool(name="out", bufs=2 * HALF_TILES))
        psum = ctx.enter_context(tc.psum_pool(name="psum", bufs=1))
        ctx.enter_context(tc.manual_schedule())

        def bank(i, shape, dtype):
            return psum.tile(shape, dtype, name="bank%d" % i, tag="bank%d" % i)

        identity_f32 = keep.tile([P, P], F32, name="identity_f32")
        identity_bf16 = keep.tile([P, P], BF16, name="identity_bf16")
        swap_halves = keep.tile([P, P], F32, name="swap_halves")
        sin_sign = keep.tile([P, 1], F32, name="sin_sign")
        bias_rows = keep.tile([P, P], BF16, name="bias_rows")
        bias_t = keep.tile([P, HEADS], F32, name="bias_t")
        cos_rows = keep.tile([P, TILES, P], BF16, name="cos_rows")
        sin_rows = keep.tile([P, TILES, P], BF16, name="sin_rows")
        tables_t = keep.tile([P, 2, 2, HALF], BF16, name="tables_t")
        x_rows = keep.tile([P, TILES * M], BF16, name="x_rows")
        x_codes = keep.tile([P, 2, PASSES, HALF], U32, name="x_codes", align_bytes=64)
        x_scales = keep.tile([P, 2, PASSES, HALF], U8, name="x_scales", align_bytes=64)
        w_codes = [keep.tile([P, PASSES, CHUNK], U32, name="w_codes%d" % j, align_bytes=64) for j in range(CHUNKS)]
        w_scales = [keep.tile([P, PASSES, CHUNK], U8, name="w_scales%d" % j, align_bytes=64) for j in range(CHUNKS)]

        def weight_sources(j):
            if j == 0:
                return (wk_dram, wv_dram)
            return (wq_dram[:, CHUNK * (j - 1) : CHUNK * j],)

        w_rows = [
            [
                keep.tile(
                    [P, len(weight_sources(j)), PACK, CHUNK // len(weight_sources(j))],
                    BF16,
                    name="w_rows%d_%d" % (j, g),
                )
                for g in range(PASSES)
            ]
            for j in range(CHUNKS)
        ]

        make_identity(nc, identity_f32[:])
        make_identity(nc, identity_bf16[:])
        nc.vector.memset(bias_rows[:], 0.0)
        nc.vector.memset(sin_sign[0 : P // 2, :], 1.0)
        nc.vector.memset(sin_sign[P // 2 : P, :], -1.0)
        nc.vector.tensor_copy(out=swap_halves[:, 0 : P // 2], in_=identity_f32[:, P // 2 : P])
        nc.vector.tensor_copy(out=swap_halves[:, P // 2 : P], in_=identity_f32[:, 0 : P // 2])

        def load_x(half):
            for t in range(HALF_TILES * half, HALF_TILES * (half + 1), 2):
                nc.sync.dma_start(
                    out=x_rows[:, t * M : (t + 2) * M],
                    in_=x_dram[:, t : t + 2, :].rearrange("p t m -> p (t m)"),
                )

        def load_weights(j):
            for g in range(PASSES):
                for u in range(2):
                    first = P * PACK * g + 2 * P * u
                    for n, source in enumerate(weight_sources(j)):
                        nc.sync.dma_start(
                            out=w_rows[j][g][:, n, 2 * u : 2 * u + 2, :],
                            in_=source[first : first + 2 * P, :].rearrange("(p e) c -> p e c", e=2),
                        )

        def load_tables(half):
            tiles = slice(HALF_TILES * half, HALF_TILES * (half + 1))
            for rows, dram, sections in ((cos_rows, cos_dram, COS_SECTIONS), (sin_rows, sin_dram, SIN_SECTIONS)):
                for component, lo, hi, column in sections:
                    source = dram[component].rearrange("(p t) d -> p t d", t=TILES)
                    nc.sync.dma_start(out=rows[:, tiles, column : column + hi - lo], in_=source[:, tiles, lo:hi])

        load_x(0)
        load_weights(0)
        nc.sync.dma_start(out=bias_rows[0:12, :], in_=bq)
        nc.sync.dma_start(out=bias_rows[12:14, :], in_=bk)
        nc.sync.dma_start(out=bias_rows[14:16, :], in_=bv)
        load_tables(0)
        load_tables(1)
        load_x(1)
        for j in range(1, CHUNKS):
            load_weights(j)

        x_grouped = {}
        w_grouped = {}
        sums = {}
        products = {}

        def bias_column(j, head):
            return 12 + head if j == 0 else CHUNK_HEADS * (j - 1) + head

        def is_rotated(j, head):
            return j > 0 or head < 2

        def transpose_x(half):
            x_words = x_rows[:].bitcast(F32)
            grouped_words = []
            for g in range(PASSES):
                grouped = x_grouped_pool.tile([P, PACK * HALF], BF16, name="x_grouped", tag="x_grouped", align_bytes=64)
                x_grouped[(half, g)] = grouped
                grouped_words.append(
                    grouped[:].bitcast(F32).rearrange("p (t s u) -> p t s u", t=HALF_TILES, u=2)
                )
            for pair in range(HALF_TILES // 2):
                for g in range(PASSES):
                    turned = bank(X_BANKS[half][PASSES * pair + g], [P, 2, 2, P], F32)
                    for t in range(2):
                        for u in range(2):
                            column = (HALF_TILES * half + 2 * pair + t) * (M // 2) + 2 * P * g + P * u
                            nc.tensor.transpose(turned[:, t, u, :], x_words[:, column : column + P], identity_f32[:])
                    nc.scalar.copy(
                        out=grouped_words[g][:, 2 * pair : 2 * pair + 2],
                        in_=turned[:].rearrange("p t u s -> p t s u"),
                    )

        def quantise_x(half, g):
            nc.vector.quantize_mx(
                out=x_codes[:, half, g, :].bitcast(FP8X4), scales=x_scales[:, half, g, :], in_=x_grouped[(half, g)][:]
            )

        def regroup_weights(copy, j, g):
            grouped = w_grouped_pool.tile([P, PACK * CHUNK], BF16, name="w_grouped", tag="w_grouped", align_bytes=64)
            w_grouped[(j, g)] = grouped
            sources = len(weight_sources(j))
            target = grouped[:].rearrange("p (n c i v) -> p n c v i", n=sources, i=4, v=PACK)
            rows = w_rows[j][g][:].rearrange("p n v (c i) -> p n c v i", i=4)
            for n in range(sources):
                copy(out=target[:, n], in_=rows[:, n])

        def quantise_weights(j, g):
            nc.vector.quantize_mx(
                out=w_codes[j][:, g, :].bitcast(FP8X4), scales=w_scales[j][:, g, :], in_=w_grouped[(j, g)][:]
            )

        def project(r, banks, pass_outer):
            j, half = divmod(r, 2)
            sums[r] = [bank(b, [P, HALF], F32) for b in banks]
            if pass_outer:
                order = [(g, head) for g in range(PASSES) for head in range(CHUNK_HEADS)]
            else:
                order = [(g, head) for head in range(CHUNK_HEADS) for g in range(PASSES)]
            for g, head in order:
                columns = slice(P * head, P * (head + 1))
                nc.tensor.matmul_mx(
                    out=sums[r][head][:],
                    lhsT=w_codes[j][:, g, columns].bitcast(FP8X4),
                    lhsT_scale=w_scales[j][:, g, columns],
                    rhs=x_codes[:, half, g, :].bitcast(FP8X4),
                    rhs_scale=x_scales[:, half, g, :],
                    start=(g == 0),
                    stop=(g == PASSES - 1),
                )

        def transpose_biases():
            turned = bank(BIAS_BANK, [P, P], BF16)
            nc.tensor.transpose(turned[:], bias_rows[:], identity_bf16[:])
            nc.vector.tensor_copy(out=bias_t[:], in_=turned[:, 0:HEADS])

        def transpose_tables(half):
            turned = bank(TABLE_BANKS[half], [P, 2, HALF], BF16)
            for table, rows in enumerate((cos_rows, sin_rows)):
                for t in range(HALF_TILES):
                    nc.tensor.transpose(
                        turned[:, table, P * t : P * (t + 1)], rows[:, HALF_TILES * half + t, :], identity_bf16[:]
                    )
            nc.scalar.copy(out=tables_t[:, half, 0, :], in_=turned[:, 0, :])
            nc.scalar.activation(out=tables_t[:, half, 1, :], in_=turned[:, 1, :], func=ACT.Copy, scale=sin_sign[:, 0:1])

        def add_bias_and_multiply(r, between):
            j, half = divmod(r, 2)
            products[r] = []
            for head in range(CHUNK_HEADS):
                bias = bias_t[:, bias_column(j, head) : bias_column(j, head) + 1]
                uw = uw_pool.tile([P, 2, HALF], F32, name="uw%d" % head, tag="uw%d" % head)
                products[r].append(uw)
                if is_rotated(j, head):
                    nc.vector.scalar_tensor_tensor(
                        out=uw[:],
                        in0=sums[r][head][:].unsqueeze(1).to_broadcast([P, 2, HALF]),
                        scalar=bias,
                        in1=tables_t[:, half],
                        op0=ADD,
                        op1=MULT,
                    )
                else:
                    nc.scalar.activation(out=uw[:, 0, :], in_=sums[r][head][:], func=ACT.Identity, bias=bias)
                for stage, a, b in between[head]:
                    stage(a, b)

        def turn_back_and_store(r):
            j, half = divmod(r, 2)
            for t in range(HALF_TILES):
                result = bank(LOW_BANKS[t], [P, CHUNK], F32)
                rows = slice(P * t, P * (t + 1))
                for head in range(CHUNK_HEADS):
                    target = result[:, P * head : P * (head + 1)]
                    uw = products[r][head]
                    if is_rotated(j, head):
                        nc.tensor.matmul(
                            out=target, lhsT=uw[:, 0, rows], rhs=identity_f32[:], is_transpose=True, start=True, stop=False
                        )
                        nc.tensor.matmul(
                            out=target, lhsT=uw[:, 1, rows], rhs=swap_halves[:], is_transpose=True, start=False, stop=True
                        )
                    else:
                        nc.tensor.transpose(target, uw[:, 0, rows], identity_f32[:])
                leaving = out_pool.tile([P, CHUNK], F32, name="leaving", tag="leaving")
                nc.scalar.copy(out=leaving[:], in_=result[:])
                tile = HALF_TILES * half + t
                if j == 0:
                    nc.sync.dma_start(out=k_dram[:, tile, :], in_=leaving[:, 0 : CHUNK // 2])
                    nc.sync.dma_start(out=v_dram[:, tile, :], in_=leaving[:, CHUNK // 2 : CHUNK])
                else:
                    nc.sync.dma_start(out=q_dram[:, tile, CHUNK * (j - 1) : CHUNK * j], in_=leaving[:])

        def regroup_on_vector(j, g):
            regroup_weights(nc.vector.tensor_copy, j, g)

        transpose_x(0)
        for g in range(PASSES):
            regroup_on_vector(0, g)
            quantise_x(0, g)
            if g > 0:
                quantise_weights(0, g - 1)
        quantise_weights(0, PASSES - 1)
        project(0, LOW_BANKS, True)
        transpose_biases()
        transpose_tables(0)
        transpose_tables(1)
        add_bias_and_multiply(0, NOTHING_BETWEEN)
        transpose_x(1)
        for g in range(PASSES):
            quantise_x(1, g)
        project(1, HIGH_BANKS, False)

        for r in range(ROUNDS):
            due = [
                (j, g) for j in range(1, CHUNKS) for g in range(PASSES) if r == max(0, 2 * j - 3 + g // 2)
            ]
            between = [[] for head in range(CHUNK_HEADS)]
            for n, (j, g) in enumerate(due):
                if len(due) == PASSES and n == 1:
                    between[0].append((regroup_on_vector, j, g))
                else:
                    regroup_weights(nc.scalar.copy, j, g)
                between[n + 1].append((quantise_weights, j, g))
            turn_back_and_store(r)
            if r + 1 < ROUNDS:
                add_bias_and_multiply(r + 1, between)
            if r + 2 < ROUNDS:
                project(r + 2, HIGH_BANKS, False)
